import numpy as np
import ml_dtypes


def mxq(x, axis, fmt="e4m3"):
    dtype, down = {"e4m3": (ml_dtypes.float8_e4m3fn, 7), "e5m2": (ml_dtypes.float8_e5m2, 14)}[fmt]
    v = np.moveaxis(np.asarray(x, np.float32).astype(ml_dtypes.bfloat16).astype(np.float64), axis, -1)
    blocks = v.reshape(v.shape[:-1] + (-1, 32))
    amax = np.abs(blocks).max(-1, keepdims=True)
    byte = np.maximum(np.where(amax > 0, np.frexp(amax)[1] - 1 + 127, 0) - down, 1)
    scale = np.exp2(byte - 127.0)
    codes = (blocks / scale).astype(np.float32).astype(dtype).astype(np.float64)
    return np.moveaxis((codes * scale).reshape(v.shape), -1, axis)


WIDE = False


def mx_kscale(k):
    if not WIDE:
        return np.ones(k)
    levels = np.array([10, -10, 5, -5, 0])
    a = np.random.permutation(np.resize(levels, k // 512 * 4)).reshape(k // 512, 4)
    idx = np.arange(k)
    return np.exp2(a[idx // 512, idx % 128 // 32])


BF16 = ml_dtypes.bfloat16


def bf(x):
    return np.asarray(x, np.float32).astype(BF16)


def f64(x):
    return np.asarray(x).astype(np.float64)


E2M1 = np.array([0.0, 0.5, 1.0, 1.5, 2.0, 3.0, 4.0, 6.0, -0.0, -0.5, -1.0, -1.5, -2.0, -3.0, -4.0, -6.0])


def pack_weight(w, fmt):
    k, n = w.shape
    w = f64(bf(w)).reshape(k // 32, 32, n)
    amax = np.abs(w).max(1)
    if fmt == "e4m3":
        byte = np.frexp(amax)[1] - 1 + 127 - 7
    else:
        mant, ex = np.frexp(amax / 6.0)
        byte = np.where(mant > 0.5, ex, ex - 1) + 127
    byte = np.clip(np.where(amax > 0, byte, 1), 1, 254)
    scaled = (w * np.exp2(127.0 - byte)[:, None, :]).reshape(k, n).astype(np.float32)
    by_word = np.ascontiguousarray(scaled.reshape(k // 512, 128, 4, n).transpose(0, 1, 3, 2))
    if fmt == "e4m3":
        words = by_word.astype(ml_dtypes.float8_e4m3fn).view(np.uint8)
    else:
        c = by_word.astype(ml_dtypes.float4_e2m1fn).view(np.uint8) & 0xF
        words = c[..., 0::2] | (c[..., 1::2] << 4)
    return np.ascontiguousarray(words), np.ascontiguousarray(byte.astype(np.uint8).reshape(k // 512, 16, n))


def unpack_weight(words, scales, fmt):
    g, p, n, _ = words.shape
    if fmt == "e4m3":
        vals = np.ascontiguousarray(words).view(ml_dtypes.float8_e4m3fn).astype(np.float64)
    else:
        nib = np.empty((g, p, n, 4), np.uint8)
        nib[..., 0::2] = words & 0xF
        nib[..., 1::2] = words >> 4
        vals = E2M1[nib]
    vals = vals * np.repeat(np.exp2(scales.astype(np.float64) - 127.0), 8, axis=1)[..., None]
    return vals.transpose(0, 1, 3, 2).reshape(g * 512, n)

def pack4(w):
    words, scales = pack_weight(w, "e2m1")
    return words.reshape(words.shape[0], 128, -1), scales


def unpack4(words, scales):
    return unpack_weight(words.reshape(words.shape[0], 128, -1, 2), scales, "e2m1")


B, N, K, H, C_E, M = 2, 256, 32, 256, 1024, 512
SCALE = 30.0


def setup_inputs():
    s = mx_kscale(M)
    h2 = bf(np.random.standard_normal((B, N, K, M)) * 0.65 * s)
    h_V = bf(np.random.standard_normal((B, N, H)))
    mask_attend = bf(np.random.uniform(size=(B, N, K)) < 0.9)
    words, scales = pack4(np.random.standard_normal((M, H)) * 4.0 / np.sqrt(M) / s[:, None])
    W3_b = bf(np.random.standard_normal(H) * 0.1)
    return {"h2": h2,
            "h_V": h_V,
            "mask_attend": mask_attend,
            "W3_w_words": words,
            "W3_w_scales": scales,
            "W3_b": W3_b}


def reference(h2, h_V, mask_attend, W3_w_words, W3_w_scales, W3_b):
    h_message = (mxq(f64(h2), 3, "e4m3") @ unpack4(W3_w_words, W3_w_scales)) + f64(W3_b)
    h_message = f64(mask_attend)[..., None] * h_message
    dh = np.sum(h_message, axis=-2) / SCALE
    return f64(h_V) + dh

@@ -1,0 +1,221 @@
+from contextlib import ExitStack
+
+import concourse.mybir as mybir
+from concourse.masks import make_identity
+
+BF16 = mybir.dt.bfloat16
+F32 = mybir.dt.float32
+I32 = mybir.dt.int32
+U32 = mybir.dt.uint32
+U8 = mybir.dt.uint8
+FP8X4 = mybir.dt.float8_e4m3fn_x4
+FP4X4 = mybir.dt.float4_e2m1fn_x4
+MULT = mybir.AluOpType.mult
+ADD = mybir.AluOpType.add
+
+P = 128
+NODES = 512
+EDGES = 32
+K = 512
+H = 256
+SCALE = 30.0
+NODE_TILES = NODES // P
+H_HALVES = H // P
+
+LOAD_EDGES = 4
+ROUND = 8
+ROUNDS_PER_TILE = EDGES // ROUND
+ROUNDS = NODE_TILES * ROUNDS_PER_TILE
+LOADS = NODE_TILES * EDGES // LOAD_EDGES
+BANK_UNITS = 2
+ROUND_BANKS = ROUND // BANK_UNITS
+QUANT_UNITS = 4
+TRANSPOSE_BANKS = 6
+
+FLOPS = 2 * NODES * EDGES * K * H
+
+
+def tile_declayerj_pb_t_kernel(
+    tc, h2, h_V, mask_attend, W3_w_words, W3_w_scales, W3_b, out
+):
+    nc = tc.nc
+    x_rows = h2.rearrange("b n k m -> (b n) (k m)")
+    hv_rows = h_V.rearrange("b n h -> (b n) h")
+    mask_rows = mask_attend.rearrange("b n k -> (b n) k")
+    out_rows = out.rearrange("b n h -> (b n) h")
+
+    with ExitStack() as ctx:
+        ctx.enter_context(tc.manual_schedule())
+        const = ctx.enter_context(tc.tile_pool(name="const", bufs=1))
+        x_pool = ctx.enter_context(tc.tile_pool(name="x", bufs=LOADS))
+        sorted_pool = ctx.enter_context(tc.tile_pool(name="sorted", bufs=3))
+        grouped_pool = ctx.enter_context(tc.tile_pool(name="grouped", bufs=2))
+        codes_pool = ctx.enter_context(tc.tile_pool(name="codes", bufs=2))
+        out_pool = ctx.enter_context(tc.tile_pool(name="result", bufs=NODE_TILES))
+        bank_pool = ctx.enter_context(tc.psum_pool(name="banks", bufs=TRANSPOSE_BANKS))
+        acc_pool = ctx.enter_context(tc.psum_pool(name="acc", bufs=1))
+
+        mask_bf = const.tile([P, NODE_TILES, EDGES], BF16)
+        nc.sync.dma_start(out=mask_bf[:], in_=mask_rows.rearrange("(j p) k -> p j k", p=P))
+
+        x_tiles = []
+
+        def load_x(first, last):
+            for c in range(first, last):
+                j, e0 = divmod(c * LOAD_EDGES, EDGES)
+                x_t = x_pool.tile([P, LOAD_EDGES, K], BF16, name="x_t")
+                nc.sync.dma_start(
+                    out=x_t[:].rearrange("p e m -> p (e m)"),
+                    in_=x_rows[j * P : (j + 1) * P, e0 * K : (e0 + LOAD_EDGES) * K],
+                )
+                x_tiles.append(x_t)
+
+        load_x(0, ROUND // LOAD_EDGES)
+
+        w_plane = const.tile([P, H], U8, align_bytes=64)
+        nc.vector.memset(w_plane[:].bitcast(I32), 0)
+        for quadrant in range(4):
+            nc.sync.dma_start(
+                out=w_plane[32 * quadrant : 32 * quadrant + 4, :].bitcast(I32),
+                in_=W3_w_scales[0, 4 * quadrant : 4 * quadrant + 4, :].bitcast(I32),
+            )
+        w_words = const.tile([P, 2 * H], U8, align_bytes=64)
+        nc.sync.dma_start(out=w_words[:].bitcast(I32), in_=W3_w_words[0].bitcast(I32))
+
+        bias_row = const.tile([P, H], BF16)
+        nc.vector.memset(bias_row[:], 0.0)
+        nc.sync.dma_start(out=bias_row[0:1, :], in_=W3_b.unsqueeze(0))
+        hv = const.tile([P, NODE_TILES, H], BF16)
+        nc.sync.dma_start(out=hv[:], in_=hv_rows.rearrange("(j p) h -> p j h", p=P))
+
+        load_x(ROUND // LOAD_EDGES, LOADS)
+
+        ident = const.tile([P, P], F32)
+        make_identity(nc, ident[:])
+        ones = const.tile([P, P], BF16)
+        nc.vector.memset(ones[:], 1.0)
+        mask_f32 = const.tile([P, NODE_TILES, EDGES], F32)
+        nc.vector.tensor_copy(out=mask_f32[:], in_=mask_bf[:])
+        count = const.tile([P, NODE_TILES], F32)
+        nc.vector.tensor_reduce(out=count[:], in_=mask_f32[:], axis=mybir.AxisListType.X, op=ADD)
+        count_scaled = const.tile([P, NODE_TILES], F32)
+        nc.vector.tensor_scalar(
+            out=count_scaled[:], in0=count[:], scalar1=1.0 / SCALE, scalar2=None, op0=MULT
+        )
+        base = const.tile([P, NODE_TILES, H], F32)
+
+        sorted_tiles = {}
+        grouped_tiles = {}
+        codes_tiles = {}
+        acc_tiles = {}
+
+        def mask_and_sort(r):
+            j, e0 = divmod(r * ROUND, EDGES)
+            sorted_t = sorted_pool.tile([P, ROUND, K], BF16, name="sorted_t")
+            for i in range(ROUND):
+                x_t = x_tiles[(r * ROUND + i) // LOAD_EDGES]
+                nc.vector.tensor_scalar(
+                    out=sorted_t[:, i, :].rearrange("p (u q t) -> p u q t", u=2, t=2),
+                    in0=x_t[:, i % LOAD_EDGES, :].rearrange("p (q u t) -> p u q t", u=2, t=2),
+                    scalar1=mask_f32[:, j, e0 + i : e0 + i + 1],
+                    scalar2=None,
+                    op0=MULT,
+                )
+            sorted_tiles[r] = sorted_t
+
+        def transpose_and_group(r):
+            words = sorted_tiles[r][:].bitcast(F32)
+            grouped_t = grouped_pool.tile([P, ROUND, K], BF16, name="grouped_t", align_bytes=64)
+            grouped_words = grouped_t[:].bitcast(F32)
+            for b in range(ROUND_BANKS):
+                bank = bank_pool.tile([P, 2 * BANK_UNITS * P], F32, name="bank")
+                for a in range(BANK_UNITS):
+                    for u in range(2):
+                        s = 2 * a + u
+                        nc.tensor.transpose(
+                            out=bank[:, s * P : (s + 1) * P],
+                            in_=words[:, b * BANK_UNITS + a, u * P : (u + 1) * P],
+                            identity=ident[:],
+                        )
+                nc.scalar.copy(
+                    out=grouped_words[:, b * BANK_UNITS : (b + 1) * BANK_UNITS, :].rearrange(
+                        "p a (n u) -> p a n u", u=2
+                    ),
+                    in_=bank[:].rearrange("p (a u n) -> p a n u", a=BANK_UNITS, u=2),
+                )
+            grouped_tiles[r] = grouped_t
+
+        def quantise(r):
+            grouped_t = grouped_tiles[r]
+            codes = codes_pool.tile([P, ROUND * P], U32, name="codes", align_bytes=64)
+            scales = codes_pool.tile([P, ROUND * P], U8, name="scales", align_bytes=64)
+            for g in range(ROUND // QUANT_UNITS):
+                cols = slice(g * QUANT_UNITS * P, (g + 1) * QUANT_UNITS * P)
+                nc.vector.quantize_mx(
+                    out=codes[:, cols].bitcast(FP8X4),
+                    scales=scales[:, cols],
+                    in_=grouped_t[:, g * QUANT_UNITS : (g + 1) * QUANT_UNITS, :].rearrange(
+                        "p a c -> p (a c)"
+                    ),
+                )
+            codes_tiles[r] = (codes, scales)
+
+        def multiply(r):
+            j, e0 = divmod(r * ROUND, EDGES)
+            codes, scales = codes_tiles[r]
+            if e0 == 0:
+                acc_tiles[j] = [
+                    acc_pool.tile([P, P], F32, name="acc%d" % half) for half in range(H_HALVES)
+                ]
+            for i in range(ROUND):
+                for half in range(H_HALVES):
+                    nc.tensor.matmul_mx(
+                        out=acc_tiles[j][half][:],
+                        lhsT=codes[:, i * P : (i + 1) * P].bitcast(FP8X4),
+                        lhsT_scale=scales[:, i * P : (i + 1) * P],
+                        rhs=w_words[:, half * 2 * P : (half + 1) * 2 * P].bitcast(FP4X4),
+                        rhs_scale=w_plane[:, half * P : (half + 1) * P],
+                        start=(e0 + i == 0),
+                        stop=(e0 + i == EDGES - 1),
+                    )
+
+        def finish_tile(j):
+            result = out_pool.tile([P, H], F32, name="result")
+            for half, acc in enumerate(acc_tiles[j]):
+                cols = slice(half * P, (half + 1) * P)
+                nc.vector.scalar_tensor_tensor(
+                    out=result[:, cols],
+                    in0=acc[:],
+                    scalar=1.0 / SCALE,
+                    in1=base[:, j, cols],
+                    op0=MULT,
+                    op1=ADD,
+                )
+            nc.sync.dma_start(out=out_rows[j * P : (j + 1) * P, :], in_=result[:])
+
+        mask_and_sort(0)
+        transpose_and_group(0)
+
+        bias_bank = bank_pool.tile([P, 2 * BANK_UNITS * P], F32, name="bank")
+        nc.tensor.matmul(out=bias_bank[:, :H], lhsT=ones[:], rhs=bias_row[:], start=True, stop=True)
+        for j in range(NODE_TILES):
+            nc.vector.scalar_tensor_tensor(
+                out=base[:, j, :],
+                in0=bias_bank[:, :H],
+                scalar=count_scaled[:, j : j + 1],
+                in1=hv[:, j, :],
+                op0=MULT,
+                op1=ADD,
+            )
+
+        mask_and_sort(1)
+        for r in range(ROUNDS):
+            if r > 0 and r % ROUNDS_PER_TILE == 0:
+                finish_tile(r // ROUNDS_PER_TILE - 1)
+            quantise(r)
+            if r + 2 < ROUNDS:
+                mask_and_sort(r + 2)
+            if r + 1 < ROUNDS:
+                transpose_and_group(r + 1)
+            multiply(r)
+        finish_tile(NODE_TILES - 1)

@@ -115,8 +115,8 @@ def tile_declayerj_pb_t_kernel(
             for i in range(ROUND):
                 x_t = x_tiles[(r * ROUND + i) // LOAD_EDGES]
                 nc.vector.tensor_scalar(
-                    out=sorted_t[:, i, :].rearrange("p (u q t) -> p u q t", u=2, t=2),
-                    in0=x_t[:, i % LOAD_EDGES, :].rearrange("p (q u t) -> p u q t", u=2, t=2),
+                    out=sorted_t[:, i, :].rearrange("p (u q t) -> p q u t", u=2, t=2),
+                    in0=x_t[:, i % LOAD_EDGES, :].rearrange("p (q u t) -> p q u t", u=2, t=2),
                     scalar1=mask_f32[:, j, e0 + i : e0 + i + 1],
                     scalar2=None,
                     op0=MULT,

@@ -21,16 +21,16 @@ H = 256
 SCALE = 30.0
 NODE_TILES = NODES // P
 H_HALVES = H // P
+UNITS = NODE_TILES * EDGES
 
-LOAD_EDGES = 4
-ROUND = 8
-ROUNDS_PER_TILE = EDGES // ROUND
-ROUNDS = NODE_TILES * ROUNDS_PER_TILE
-LOADS = NODE_TILES * EDGES // LOAD_EDGES
+LOAD_PLAN = [[1, 1, 2] + [4] * 7] + [[4] * 8] * 3
+GROUP_PLAN = [[2, 2, 4, 8, 8, 8]] + [[8] * 4] * 3
 BANK_UNITS = 2
-ROUND_BANKS = ROUND // BANK_UNITS
 QUANT_UNITS = 4
 TRANSPOSE_BANKS = 6
+SORTED_BUFS = 14
+GROUPED_BUFS = 5
+CODES_BUFS = 6
 
 FLOPS = 2 * NODES * EDGES * K * H
 
@@ -44,33 +44,49 @@ def tile_declayerj_pb_t_kernel(
     mask_rows = mask_attend.rearrange("b n k -> (b n) k")
     out_rows = out.rearrange("b n h -> (b n) h")
 
+    assert all(sum(plan) == EDGES for plan in LOAD_PLAN) and len(LOAD_PLAN) == NODE_TILES
+    assert all(sum(plan) == EDGES for plan in GROUP_PLAN) and len(GROUP_PLAN) == NODE_TILES
+    loads = []
+    groups = []
+    for j in range(NODE_TILES):
+        first = j * EDGES
+        for n in LOAD_PLAN[j]:
+            loads.append((first, n))
+            first += n
+        first = j * EDGES
+        for n in GROUP_PLAN[j]:
+            groups.append((first, n))
+            first += n
+
     with ExitStack() as ctx:
         ctx.enter_context(tc.manual_schedule())
         const = ctx.enter_context(tc.tile_pool(name="const", bufs=1))
-        x_pool = ctx.enter_context(tc.tile_pool(name="x", bufs=LOADS))
-        sorted_pool = ctx.enter_context(tc.tile_pool(name="sorted", bufs=3))
-        grouped_pool = ctx.enter_context(tc.tile_pool(name="grouped", bufs=2))
-        codes_pool = ctx.enter_context(tc.tile_pool(name="codes", bufs=2))
+        x_pool = ctx.enter_context(tc.tile_pool(name="x", bufs=1))
+        sorted_pool = ctx.enter_context(tc.tile_pool(name="sorted", bufs=SORTED_BUFS))
+        grouped_pool = ctx.enter_context(tc.tile_pool(name="grouped", bufs=GROUPED_BUFS))
+        codes_pool = ctx.enter_context(tc.tile_pool(name="codes", bufs=CODES_BUFS))
         out_pool = ctx.enter_context(tc.tile_pool(name="result", bufs=NODE_TILES))
         bank_pool = ctx.enter_context(tc.psum_pool(name="banks", bufs=TRANSPOSE_BANKS))
         acc_pool = ctx.enter_context(tc.psum_pool(name="acc", bufs=1))
 
         mask_bf = const.tile([P, NODE_TILES, EDGES], BF16)
-        nc.sync.dma_start(out=mask_bf[:], in_=mask_rows.rearrange("(j p) k -> p j k", p=P))
+        nc.scalar.dma_start(out=mask_bf[:], in_=mask_rows.rearrange("(j p) k -> p j k", p=P))
 
-        x_tiles = []
+        x_of_unit = {}
 
-        def load_x(first, last):
-            for c in range(first, last):
-                j, e0 = divmod(c * LOAD_EDGES, EDGES)
-                x_t = x_pool.tile([P, LOAD_EDGES, K], BF16, name="x_t")
+        def load_x(first_load, last_load):
+            for c in range(first_load, last_load):
+                first, n = loads[c]
+                j, e0 = divmod(first, EDGES)
+                x_t = x_pool.tile([P, n, K], BF16, name="x%d" % c)
                 nc.sync.dma_start(
                     out=x_t[:].rearrange("p e m -> p (e m)"),
-                    in_=x_rows[j * P : (j + 1) * P, e0 * K : (e0 + LOAD_EDGES) * K],
+                    in_=x_rows[j * P : (j + 1) * P, e0 * K : (e0 + n) * K],
                 )
-                x_tiles.append(x_t)
+                for i in range(n):
+                    x_of_unit[first + i] = x_t[:, i, :]
 
-        load_x(0, ROUND // LOAD_EDGES)
+        load_x(0, 3)
 
         w_plane = const.tile([P, H], U8, align_bytes=64)
         nc.vector.memset(w_plane[:].bitcast(I32), 0)
@@ -84,11 +100,11 @@ def tile_declayerj_pb_t_kernel(
 
         bias_row = const.tile([P, H], BF16)
         nc.vector.memset(bias_row[:], 0.0)
-        nc.sync.dma_start(out=bias_row[0:1, :], in_=W3_b.unsqueeze(0))
+        nc.scalar.dma_start(out=bias_row[0:1, :], in_=W3_b.unsqueeze(0))
         hv = const.tile([P, NODE_TILES, H], BF16)
-        nc.sync.dma_start(out=hv[:], in_=hv_rows.rearrange("(j p) h -> p j h", p=P))
+        nc.scalar.dma_start(out=hv[:], in_=hv_rows.rearrange("(j p) h -> p j h", p=P))
 
-        load_x(ROUND // LOAD_EDGES, LOADS)
+        load_x(3, len(loads))
 
         ident = const.tile([P, P], F32)
         make_identity(nc, ident[:])
@@ -97,87 +113,89 @@ def tile_declayerj_pb_t_kernel(
         mask_f32 = const.tile([P, NODE_TILES, EDGES], F32)
         nc.vector.tensor_copy(out=mask_f32[:], in_=mask_bf[:])
         count = const.tile([P, NODE_TILES], F32)
-        nc.vector.tensor_reduce(out=count[:], in_=mask_f32[:], axis=mybir.AxisListType.X, op=ADD)
         count_scaled = const.tile([P, NODE_TILES], F32)
-        nc.vector.tensor_scalar(
-            out=count_scaled[:], in0=count[:], scalar1=1.0 / SCALE, scalar2=None, op0=MULT
-        )
         base = const.tile([P, NODE_TILES, H], F32)
 
-        sorted_tiles = {}
-        grouped_tiles = {}
-        codes_tiles = {}
+        sorted_of_bank = {}
+        chunks_of_group = {}
+        codes_of_group = {}
         acc_tiles = {}
 
-        def mask_and_sort(r):
-            j, e0 = divmod(r * ROUND, EDGES)
-            sorted_t = sorted_pool.tile([P, ROUND, K], BF16, name="sorted_t")
-            for i in range(ROUND):
-                x_t = x_tiles[(r * ROUND + i) // LOAD_EDGES]
+        def mask_and_sort(g):
+            first, n = groups[g]
+            for u in range(first, first + n):
+                j, e = divmod(u, EDGES)
+                if u % BANK_UNITS == 0:
+                    sorted_t = sorted_pool.tile([P, BANK_UNITS, K], BF16, name="sorted_t")
+                    sorted_of_bank[u // BANK_UNITS] = sorted_t
                 nc.vector.tensor_scalar(
-                    out=sorted_t[:, i, :].rearrange("p (u q t) -> p q u t", u=2, t=2),
-                    in0=x_t[:, i % LOAD_EDGES, :].rearrange("p (q u t) -> p q u t", u=2, t=2),
-                    scalar1=mask_f32[:, j, e0 + i : e0 + i + 1],
+                    out=sorted_of_bank[u // BANK_UNITS][:, u % BANK_UNITS, :].rearrange(
+                        "p (u q t) -> p q u t", u=2, t=2
+                    ),
+                    in0=x_of_unit[u].rearrange("p (q u t) -> p q u t", u=2, t=2),
+                    scalar1=mask_f32[:, j, e : e + 1],
                     scalar2=None,
                     op0=MULT,
                 )
-            sorted_tiles[r] = sorted_t
 
-        def transpose_and_group(r):
-            words = sorted_tiles[r][:].bitcast(F32)
-            grouped_t = grouped_pool.tile([P, ROUND, K], BF16, name="grouped_t", align_bytes=64)
-            grouped_words = grouped_t[:].bitcast(F32)
-            for b in range(ROUND_BANKS):
-                bank = bank_pool.tile([P, 2 * BANK_UNITS * P], F32, name="bank")
-                for a in range(BANK_UNITS):
-                    for u in range(2):
-                        s = 2 * a + u
-                        nc.tensor.transpose(
-                            out=bank[:, s * P : (s + 1) * P],
-                            in_=words[:, b * BANK_UNITS + a, u * P : (u + 1) * P],
-                            identity=ident[:],
-                        )
-                nc.scalar.copy(
-                    out=grouped_words[:, b * BANK_UNITS : (b + 1) * BANK_UNITS, :].rearrange(
-                        "p a (n u) -> p a n u", u=2
-                    ),
-                    in_=bank[:].rearrange("p (a u n) -> p a n u", a=BANK_UNITS, u=2),
-                )
-            grouped_tiles[r] = grouped_t
-
-        def quantise(r):
-            grouped_t = grouped_tiles[r]
-            codes = codes_pool.tile([P, ROUND * P], U32, name="codes", align_bytes=64)
-            scales = codes_pool.tile([P, ROUND * P], U8, name="scales", align_bytes=64)
-            for g in range(ROUND // QUANT_UNITS):
-                cols = slice(g * QUANT_UNITS * P, (g + 1) * QUANT_UNITS * P)
-                nc.vector.quantize_mx(
-                    out=codes[:, cols].bitcast(FP8X4),
-                    scales=scales[:, cols],
-                    in_=grouped_t[:, g * QUANT_UNITS : (g + 1) * QUANT_UNITS, :].rearrange(
-                        "p a c -> p (a c)"
-                    ),
-                )
-            codes_tiles[r] = (codes, scales)
-
-        def multiply(r):
-            j, e0 = divmod(r * ROUND, EDGES)
-            codes, scales = codes_tiles[r]
-            if e0 == 0:
-                acc_tiles[j] = [
-                    acc_pool.tile([P, P], F32, name="acc%d" % half) for half in range(H_HALVES)
-                ]
-            for i in range(ROUND):
-                for half in range(H_HALVES):
-                    nc.tensor.matmul_mx(
-                        out=acc_tiles[j][half][:],
-                        lhsT=codes[:, i * P : (i + 1) * P].bitcast(FP8X4),
-                        lhsT_scale=scales[:, i * P : (i + 1) * P],
-                        rhs=w_words[:, half * 2 * P : (half + 1) * 2 * P].bitcast(FP4X4),
-                        rhs_scale=w_plane[:, half * P : (half + 1) * P],
-                        start=(e0 + i == 0),
-                        stop=(e0 + i == EDGES - 1),
+        def transpose_and_group(g):
+            first, n = groups[g]
+            chunks = []
+            for c0 in range(first, first + n, QUANT_UNITS):
+                cn = min(QUANT_UNITS, first + n - c0)
+                grouped_t = grouped_pool.tile([P, QUANT_UNITS, K], BF16, name="grouped_t", align_bytes=64)
+                grouped_words = grouped_t[:].bitcast(F32)
+                chunks.append((c0, cn, grouped_t))
+                for b0 in range(c0, c0 + cn, BANK_UNITS):
+                    words = sorted_of_bank[b0 // BANK_UNITS][:].bitcast(F32)
+                    bank = bank_pool.tile([P, 2 * BANK_UNITS * P], F32, name="bank")
+                    for a in range(BANK_UNITS):
+                        for u in range(2):
+                            s = 2 * a + u
+                            nc.tensor.transpose(
+                                out=bank[:, s * P : (s + 1) * P],
+                                in_=words[:, a, u * P : (u + 1) * P],
+                                identity=ident[:],
+                            )
+                    nc.scalar.copy(
+                        out=grouped_words[:, b0 - c0 : b0 - c0 + BANK_UNITS, :].rearrange(
+                            "p a (n u) -> p a n u", u=2
+                        ),
+                        in_=bank[:].rearrange("p (a u n) -> p a n u", a=BANK_UNITS, u=2),
                     )
+            chunks_of_group[g] = chunks
+
+        def quantise(g):
+            made = []
+            for c0, cn, grouped_t in chunks_of_group[g]:
+                codes = codes_pool.tile([P, QUANT_UNITS * P], U32, name="codes", align_bytes=64)
+                scales = codes_pool.tile([P, QUANT_UNITS * P], U8, name="scales", align_bytes=64)
+                nc.vector.quantize_mx(
+                    out=codes[:, : cn * P].bitcast(FP8X4),
+                    scales=scales[:, : cn * P],
+                    in_=grouped_t[:, :cn, :].rearrange("p a c -> p (a c)"),
+                )
+                made.append((c0, cn, codes, scales))
+            codes_of_group[g] = made
+
+        def multiply(g):
+            for c0, cn, codes, scales in codes_of_group[g]:
+                for i in range(cn):
+                    j, e = divmod(c0 + i, EDGES)
+                    if e == 0:
+                        acc_tiles[j] = [
+                            acc_pool.tile([P, P], F32, name="acc%d" % half) for half in range(H_HALVES)
+                        ]
+                    for half in range(H_HALVES):
+                        nc.tensor.matmul_mx(
+                            out=acc_tiles[j][half][:],
+                            lhsT=codes[:, i * P : (i + 1) * P].bitcast(FP8X4),
+                            lhsT_scale=scales[:, i * P : (i + 1) * P],
+                            rhs=w_words[:, half * 2 * P : (half + 1) * 2 * P].bitcast(FP4X4),
+                            rhs_scale=w_plane[:, half * P : (half + 1) * P],
+                            start=(e == 0),
+                            stop=(e == EDGES - 1),
+                        )
 
         def finish_tile(j):
             result = out_pool.tile([P, H], F32, name="result")
@@ -193,29 +211,35 @@ def tile_declayerj_pb_t_kernel(
                 )
             nc.sync.dma_start(out=out_rows[j * P : (j + 1) * P, :], in_=result[:])
 
+        def make_base():
+            nc.vector.tensor_reduce(out=count[:], in_=mask_f32[:], axis=mybir.AxisListType.X, op=ADD)
+            nc.vector.tensor_scalar(
+                out=count_scaled[:], in0=count[:], scalar1=1.0 / SCALE, scalar2=None, op0=MULT
+            )
+            bias_bank = bank_pool.tile([P, 2 * BANK_UNITS * P], F32, name="bank")
+            nc.tensor.matmul(out=bias_bank[:, :H], lhsT=ones[:], rhs=bias_row[:], start=True, stop=True)
+            for j in range(NODE_TILES):
+                nc.vector.scalar_tensor_tensor(
+                    out=base[:, j, :],
+                    in0=bias_bank[:, :H],
+                    scalar=count_scaled[:, j : j + 1],
+                    in1=hv[:, j, :],
+                    op0=MULT,
+                    op1=ADD,
+                )
+
         mask_and_sort(0)
         transpose_and_group(0)
-
-        bias_bank = bank_pool.tile([P, 2 * BANK_UNITS * P], F32, name="bank")
-        nc.tensor.matmul(out=bias_bank[:, :H], lhsT=ones[:], rhs=bias_row[:], start=True, stop=True)
-        for j in range(NODE_TILES):
-            nc.vector.scalar_tensor_tensor(
-                out=base[:, j, :],
-                in0=bias_bank[:, :H],
-                scalar=count_scaled[:, j : j + 1],
-                in1=hv[:, j, :],
-                op0=MULT,
-                op1=ADD,
-            )
-
         mask_and_sort(1)
-        for r in range(ROUNDS):
-            if r > 0 and r % ROUNDS_PER_TILE == 0:
-                finish_tile(r // ROUNDS_PER_TILE - 1)
-            quantise(r)
-            if r + 2 < ROUNDS:
-                mask_and_sort(r + 2)
-            if r + 1 < ROUNDS:
-                transpose_and_group(r + 1)
-            multiply(r)
+        make_base()
+        for g in range(len(groups)):
+            first, n = groups[g]
+            if first > 0 and first % EDGES == 0:
+                finish_tile(first // EDGES - 1)
+            quantise(g)
+            if g + 2 < len(groups):
+                mask_and_sort(g + 2)
+            if g + 1 < len(groups):
+                transpose_and_group(g + 1)
+            multiply(g)
         finish_tile(NODE_TILES - 1)

@@ -24,13 +24,13 @@ H_HALVES = H // P
 UNITS = NODE_TILES * EDGES
 
 LOAD_PLAN = [[1, 1, 2] + [4] * 7] + [[4] * 8] * 3
-GROUP_PLAN = [[2, 2, 4, 8, 8, 8]] + [[8] * 4] * 3
+GROUP_PLAN = [[2, 2, 4, 8, 8, 8], [8, 12, 12], [12, 12, 8], [12, 12, 8]]
 BANK_UNITS = 2
 QUANT_UNITS = 4
 TRANSPOSE_BANKS = 6
-SORTED_BUFS = 14
-GROUPED_BUFS = 5
-CODES_BUFS = 6
+SORTED_BUFS = 16
+GROUPED_BUFS = 7
+CODES_BUFS = 7
 
 FLOPS = 2 * NODES * EDGES * K * H
 

@@ -31,6 +31,7 @@ TRANSPOSE_BANKS = 6
 SORTED_BUFS = 16
 GROUPED_BUFS = 7
 CODES_BUFS = 7
+WARM_UPS = 24
 
 FLOPS = 2 * NODES * EDGES * K * H
 
@@ -68,6 +69,12 @@ def tile_declayerj_pb_t_kernel(
         out_pool = ctx.enter_context(tc.tile_pool(name="result", bufs=NODE_TILES))
         bank_pool = ctx.enter_context(tc.psum_pool(name="banks", bufs=TRANSPOSE_BANKS))
         acc_pool = ctx.enter_context(tc.psum_pool(name="acc", bufs=1))
+
+        ones = const.tile([P, P], BF16)
+        nc.vector.memset(ones[:], 1.0)
+        warm_bank = bank_pool.tile([P, 2 * BANK_UNITS * P], F32, name="bank")
+        for i in range(WARM_UPS):
+            nc.tensor.matmul(out=warm_bank[:, :P], lhsT=ones[:], rhs=ones[:], start=True, stop=True)
 
         mask_bf = const.tile([P, NODE_TILES, EDGES], BF16)
         nc.scalar.dma_start(out=mask_bf[:], in_=mask_rows.rearrange("(j p) k -> p j k", p=P))
@@ -108,10 +115,6 @@ def tile_declayerj_pb_t_kernel(
 
         ident = const.tile([P, P], F32)
         make_identity(nc, ident[:])
-        ones = const.tile([P, P], BF16)
-        nc.vector.memset(ones[:], 1.0)
-        mask_f32 = const.tile([P, NODE_TILES, EDGES], F32)
-        nc.vector.tensor_copy(out=mask_f32[:], in_=mask_bf[:])
         count = const.tile([P, NODE_TILES], F32)
         count_scaled = const.tile([P, NODE_TILES], F32)
         base = const.tile([P, NODE_TILES, H], F32)
@@ -133,7 +136,7 @@ def tile_declayerj_pb_t_kernel(
                         "p (u q t) -> p q u t", u=2, t=2
                     ),
                     in0=x_of_unit[u].rearrange("p (q u t) -> p q u t", u=2, t=2),
-                    scalar1=mask_f32[:, j, e : e + 1],
+                    scalar1=mask_bf[:, j, e : e + 1],
                     scalar2=None,
                     op0=MULT,
                 )
@@ -178,7 +181,7 @@ def tile_declayerj_pb_t_kernel(
                 made.append((c0, cn, codes, scales))
             codes_of_group[g] = made
 
-        def multiply(g):
+        def multiply(g, halves):
             for c0, cn, codes, scales in codes_of_group[g]:
                 for i in range(cn):
                     j, e = divmod(c0 + i, EDGES)
@@ -186,7 +189,7 @@ def tile_declayerj_pb_t_kernel(
                         acc_tiles[j] = [
                             acc_pool.tile([P, P], F32, name="acc%d" % half) for half in range(H_HALVES)
                         ]
-                    for half in range(H_HALVES):
+                    for half in halves:
                         nc.tensor.matmul_mx(
                             out=acc_tiles[j][half][:],
                             lhsT=codes[:, i * P : (i + 1) * P].bitcast(FP8X4),
@@ -197,22 +200,25 @@ def tile_declayerj_pb_t_kernel(
                             stop=(e == EDGES - 1),
                         )
 
+        def finish_half(j, half, result):
+            cols = slice(half * P, (half + 1) * P)
+            nc.vector.scalar_tensor_tensor(
+                out=result[:, cols],
+                in0=acc_tiles[j][half][:],
+                scalar=1.0 / SCALE,
+                in1=base[:, j, cols],
+                op0=MULT,
+                op1=ADD,
+            )
+
         def finish_tile(j):
             result = out_pool.tile([P, H], F32, name="result")
-            for half, acc in enumerate(acc_tiles[j]):
-                cols = slice(half * P, (half + 1) * P)
-                nc.vector.scalar_tensor_tensor(
-                    out=result[:, cols],
-                    in0=acc[:],
-                    scalar=1.0 / SCALE,
-                    in1=base[:, j, cols],
-                    op0=MULT,
-                    op1=ADD,
-                )
+            for half in range(H_HALVES):
+                finish_half(j, half, result)
             nc.sync.dma_start(out=out_rows[j * P : (j + 1) * P, :], in_=result[:])
 
         def make_base():
-            nc.vector.tensor_reduce(out=count[:], in_=mask_f32[:], axis=mybir.AxisListType.X, op=ADD)
+            nc.vector.tensor_reduce(out=count[:], in_=mask_bf[:], axis=mybir.AxisListType.X, op=ADD)
             nc.vector.tensor_scalar(
                 out=count_scaled[:], in0=count[:], scalar1=1.0 / SCALE, scalar2=None, op0=MULT
             )
@@ -241,5 +247,13 @@ def tile_declayerj_pb_t_kernel(
                 mask_and_sort(g + 2)
             if g + 1 < len(groups):
                 transpose_and_group(g + 1)
-            multiply(g)
-        finish_tile(NODE_TILES - 1)
+            if g + 1 < len(groups):
+                multiply(g, range(H_HALVES))
+        last_result = out_pool.tile([P, H], F32, name="result")
+        for half in range(H_HALVES):
+            multiply(len(groups) - 1, [half])
+            finish_half(NODE_TILES - 1, half, last_result)
+            nc.sync.dma_start(
+                out=out_rows[(NODE_TILES - 1) * P :, half * P : (half + 1) * P],
+                in_=last_result[:, half * P : (half + 1) * P],
+            )

@@ -211,10 +211,22 @@ def tile_declayerj_pb_t_kernel(
                 op1=ADD,
             )
 
-        def finish_tile(j):
-            result = out_pool.tile([P, H], F32, name="result")
+        scaled_sums = {}
+
+        def empty_groups(j):
+            scaled = out_pool.tile([P, H], F32, name="scaled")
             for half in range(H_HALVES):
-                finish_half(j, half, result)
+                nc.scalar.activation(
+                    out=scaled[:, half * P : (half + 1) * P],
+                    in_=acc_tiles[j][half][:],
+                    func=mybir.ActivationFunctionType.Copy,
+                    scale=1.0 / SCALE,
+                )
+            scaled_sums[j] = scaled
+
+        def add_base_and_store(j):
+            result = out_pool.tile([P, H], F32, name="result")
+            nc.vector.tensor_tensor(out=result[:], in0=scaled_sums[j][:], in1=base[:, j, :], op=ADD)
             nc.sync.dma_start(out=out_rows[j * P : (j + 1) * P, :], in_=result[:])
 
         def make_base():
@@ -241,8 +253,11 @@ def tile_declayerj_pb_t_kernel(
         for g in range(len(groups)):
             first, n = groups[g]
             if first > 0 and first % EDGES == 0:
-                finish_tile(first // EDGES - 1)
+                empty_groups(first // EDGES - 1)
             quantise(g)
+            if g + 1 == len(groups):
+                for j in range(NODE_TILES - 1):
+                    add_base_and_store(j)
             if g + 2 < len(groups):
                 mask_and_sort(g + 2)
             if g + 1 < len(groups):

@@ -12,6 +12,7 @@ FP8X4 = mybir.dt.float8_e4m3fn_x4
 FP4X4 = mybir.dt.float4_e2m1fn_x4
 MULT = mybir.AluOpType.mult
 ADD = mybir.AluOpType.add
+AND = mybir.AluOpType.bitwise_and
 
 P = 128
 NODES = 512
@@ -31,6 +32,7 @@ TRANSPOSE_BANKS = 6
 SORTED_BUFS = 16
 GROUPED_BUFS = 7
 CODES_BUFS = 7
+SORT_RUN = 2
 WARM_UPS = 24
 
 FLOPS = 2 * NODES * EDGES * K * H
@@ -113,6 +115,8 @@ def tile_declayerj_pb_t_kernel(
 
         load_x(3, len(loads))
 
+        mask_bits = const.tile([P, NODE_TILES, EDGES], I32)
+        nc.vector.tensor_scalar(out=mask_bits[:], in0=mask_bf[:], scalar1=-1.0, scalar2=None, op0=MULT)
         ident = const.tile([P, P], F32)
         make_identity(nc, ident[:])
         count = const.tile([P, NODE_TILES], F32)
@@ -132,13 +136,13 @@ def tile_declayerj_pb_t_kernel(
                     sorted_t = sorted_pool.tile([P, BANK_UNITS, K], BF16, name="sorted_t")
                     sorted_of_bank[u // BANK_UNITS] = sorted_t
                 nc.vector.tensor_scalar(
-                    out=sorted_of_bank[u // BANK_UNITS][:, u % BANK_UNITS, :].rearrange(
-                        "p (u q t) -> p q u t", u=2, t=2
+                    out=sorted_of_bank[u // BANK_UNITS][:, u % BANK_UNITS, :].bitcast(I32).rearrange(
+                        "p (u c i) -> p c u i", u=2, i=SORT_RUN
                     ),
-                    in0=x_of_unit[u].rearrange("p (q u t) -> p q u t", u=2, t=2),
-                    scalar1=mask_bf[:, j, e : e + 1],
+                    in0=x_of_unit[u].bitcast(I32).rearrange("p (c i u) -> p c u i", i=SORT_RUN, u=2),
+                    scalar1=mask_bits[:, j, e : e + 1],
                     scalar2=None,
-                    op0=MULT,
+                    op0=AND,
                 )
 
         def transpose_and_group(g):

@@ -32,7 +32,7 @@ TRANSPOSE_BANKS = 6
 SORTED_BUFS = 16
 GROUPED_BUFS = 7
 CODES_BUFS = 7
-SORT_RUN = 2
+SORT_RUN = 4
 WARM_UPS = 24
 
 FLOPS = 2 * NODES * EDGES * K * H

from contextlib import ExitStack

import concourse.mybir as mybir
from concourse.masks import make_identity

BF16 = mybir.dt.bfloat16
F32 = mybir.dt.float32
I32 = mybir.dt.int32
U32 = mybir.dt.uint32
U8 = mybir.dt.uint8
FP8X4 = mybir.dt.float8_e4m3fn_x4
FP4X4 = mybir.dt.float4_e2m1fn_x4
MULT = mybir.AluOpType.mult
ADD = mybir.AluOpType.add
AND = mybir.AluOpType.bitwise_and

P = 128
NODES = 512
EDGES = 32
K = 512
H = 256
SCALE = 30.0
NODE_TILES = NODES // P
H_HALVES = H // P
UNITS = NODE_TILES * EDGES

LOAD_PLAN = [[1, 1, 2] + [4] * 7] + [[4] * 8] * 3
GROUP_PLAN = [[2, 2, 4, 8, 8, 8], [8, 12, 12], [12, 12, 8], [12, 12, 8]]
BANK_UNITS = 2
QUANT_UNITS = 4
TRANSPOSE_BANKS = 6
SORTED_BUFS = 16
GROUPED_BUFS = 7
CODES_BUFS = 7
SORT_RUN = 4
WARM_UPS = 24

FLOPS = 2 * NODES * EDGES * K * H


def tile_declayerj_pb_t_kernel(
    tc, h2, h_V, mask_attend, W3_w_words, W3_w_scales, W3_b, out
):
    nc = tc.nc
    x_rows = h2.rearrange("b n k m -> (b n) (k m)")
    hv_rows = h_V.rearrange("b n h -> (b n) h")
    mask_rows = mask_attend.rearrange("b n k -> (b n) k")
    out_rows = out.rearrange("b n h -> (b n) h")

    assert all(sum(plan) == EDGES for plan in LOAD_PLAN) and len(LOAD_PLAN) == NODE_TILES
    assert all(sum(plan) == EDGES for plan in GROUP_PLAN) and len(GROUP_PLAN) == NODE_TILES
    loads = []
    groups = []
    for j in range(NODE_TILES):
        first = j * EDGES
        for n in LOAD_PLAN[j]:
            loads.append((first, n))
            first += n
        first = j * EDGES
        for n in GROUP_PLAN[j]:
            groups.append((first, n))
            first += n

    with ExitStack() as ctx:
        ctx.enter_context(tc.manual_schedule())
        const = ctx.enter_context(tc.tile_pool(name="const", bufs=1))
        x_pool = ctx.enter_context(tc.tile_pool(name="x", bufs=1))
        sorted_pool = ctx.enter_context(tc.tile_pool(name="sorted", bufs=SORTED_BUFS))
        grouped_pool = ctx.enter_context(tc.tile_pool(name="grouped", bufs=GROUPED_BUFS))
        codes_pool = ctx.enter_context(tc.tile_pool(name="codes", bufs=CODES_BUFS))
        out_pool = ctx.enter_context(tc.tile_pool(name="result", bufs=NODE_TILES))
        bank_pool = ctx.enter_context(tc.psum_pool(name="banks", bufs=TRANSPOSE_BANKS))
        acc_pool = ctx.enter_context(tc.psum_pool(name="acc", bufs=1))

        ones = const.tile([P, P], BF16)
        nc.vector.memset(ones[:], 1.0)
        warm_bank = bank_pool.tile([P, 2 * BANK_UNITS * P], F32, name="bank")
        for i in range(WARM_UPS):
            nc.tensor.matmul(out=warm_bank[:, :P], lhsT=ones[:], rhs=ones[:], start=True, stop=True)

        mask_bf = const.tile([P, NODE_TILES, EDGES], BF16)
        nc.scalar.dma_start(out=mask_bf[:], in_=mask_rows.rearrange("(j p) k -> p j k", p=P))

        x_of_unit = {}

        def load_x(first_load, last_load):
            for c in range(first_load, last_load):
                first, n = loads[c]
                j, e0 = divmod(first, EDGES)
                x_t = x_pool.tile([P, n, K], BF16, name="x%d" % c)
                nc.sync.dma_start(
                    out=x_t[:].rearrange("p e m -> p (e m)"),
                    in_=x_rows[j * P : (j + 1) * P, e0 * K : (e0 + n) * K],
                )
                for i in range(n):
                    x_of_unit[first + i] = x_t[:, i, :]

        load_x(0, 3)

        w_plane = const.tile([P, H], U8, align_bytes=64)
        nc.vector.memset(w_plane[:].bitcast(I32), 0)
        for quadrant in range(4):
            nc.sync.dma_start(
                out=w_plane[32 * quadrant : 32 * quadrant + 4, :].bitcast(I32),
                in_=W3_w_scales[0, 4 * quadrant : 4 * quadrant + 4, :].bitcast(I32),
            )
        w_words = const.tile([P, 2 * H], U8, align_bytes=64)
        nc.sync.dma_start(out=w_words[:].bitcast(I32), in_=W3_w_words[0].bitcast(I32))

        bias_row = const.tile([P, H], BF16)
        nc.vector.memset(bias_row[:], 0.0)
        nc.scalar.dma_start(out=bias_row[0:1, :], in_=W3_b.unsqueeze(0))
        hv = const.tile([P, NODE_TILES, H], BF16)
        nc.scalar.dma_start(out=hv[:], in_=hv_rows.rearrange("(j p) h -> p j h", p=P))

        load_x(3, len(loads))

        mask_bits = const.tile([P, NODE_TILES, EDGES], I32)
        nc.vector.tensor_scalar(out=mask_bits[:], in0=mask_bf[:], scalar1=-1.0, scalar2=None, op0=MULT)
        ident = const.tile([P, P], F32)
        make_identity(nc, ident[:])
        count = const.tile([P, NODE_TILES], F32)
        count_scaled = const.tile([P, NODE_TILES], F32)
        base = const.tile([P, NODE_TILES, H], F32)

        sorted_of_bank = {}
        chunks_of_group = {}
        codes_of_group = {}
        acc_tiles = {}

        def mask_and_sort(g):
            first, n = groups[g]
            for u in range(first, first + n):
                j, e = divmod(u, EDGES)
                if u % BANK_UNITS == 0:
                    sorted_t = sorted_pool.tile([P, BANK_UNITS, K], BF16, name="sorted_t")
                    sorted_of_bank[u // BANK_UNITS] = sorted_t
                nc.vector.tensor_scalar(
                    out=sorted_of_bank[u // BANK_UNITS][:, u % BANK_UNITS, :].bitcast(I32).rearrange(
                        "p (u c i) -> p c u i", u=2, i=SORT_RUN
                    ),
                    in0=x_of_unit[u].bitcast(I32).rearrange("p (c i u) -> p c u i", i=SORT_RUN, u=2),
                    scalar1=mask_bits[:, j, e : e + 1],
                    scalar2=None,
                    op0=AND,
                )

        def transpose_and_group(g):
            first, n = groups[g]
            chunks = []
            for c0 in range(first, first + n, QUANT_UNITS):
                cn = min(QUANT_UNITS, first + n - c0)
                grouped_t = grouped_pool.tile([P, QUANT_UNITS, K], BF16, name="grouped_t", align_bytes=64)
                grouped_words = grouped_t[:].bitcast(F32)
                chunks.append((c0, cn, grouped_t))
                for b0 in range(c0, c0 + cn, BANK_UNITS):
                    words = sorted_of_bank[b0 // BANK_UNITS][:].bitcast(F32)
                    bank = bank_pool.tile([P, 2 * BANK_UNITS * P], F32, name="bank")
                    for a in range(BANK_UNITS):
                        for u in range(2):
                            s = 2 * a + u
                            nc.tensor.transpose(
                                out=bank[:, s * P : (s + 1) * P],
                                in_=words[:, a, u * P : (u + 1) * P],
                                identity=ident[:],
                            )
                    nc.scalar.copy(
                        out=grouped_words[:, b0 - c0 : b0 - c0 + BANK_UNITS, :].rearrange(
                            "p a (n u) -> p a n u", u=2
                        ),
                        in_=bank[:].rearrange("p (a u n) -> p a n u", a=BANK_UNITS, u=2),
                    )
            chunks_of_group[g] = chunks

        def quantise(g):
            made = []
            for c0, cn, grouped_t in chunks_of_group[g]:
                codes = codes_pool.tile([P, QUANT_UNITS * P], U32, name="codes", align_bytes=64)
                scales = codes_pool.tile([P, QUANT_UNITS * P], U8, name="scales", align_bytes=64)
                nc.vector.quantize_mx(
                    out=codes[:, : cn * P].bitcast(FP8X4),
                    scales=scales[:, : cn * P],
                    in_=grouped_t[:, :cn, :].rearrange("p a c -> p (a c)"),
                )
                made.append((c0, cn, codes, scales))
            codes_of_group[g] = made

        def multiply(g, halves):
            for c0, cn, codes, scales in codes_of_group[g]:
                for i in range(cn):
                    j, e = divmod(c0 + i, EDGES)
                    if e == 0:
                        acc_tiles[j] = [
                            acc_pool.tile([P, P], F32, name="acc%d" % half) for half in range(H_HALVES)
                        ]
                    for half in halves:
                        nc.tensor.matmul_mx(
                            out=acc_tiles[j][half][:],
                            lhsT=codes[:, i * P : (i + 1) * P].bitcast(FP8X4),
                            lhsT_scale=scales[:, i * P : (i + 1) * P],
                            rhs=w_words[:, half * 2 * P : (half + 1) * 2 * P].bitcast(FP4X4),
                            rhs_scale=w_plane[:, half * P : (half + 1) * P],
                            start=(e == 0),
                            stop=(e == EDGES - 1),
                        )

        def finish_half(j, half, result):
            cols = slice(half * P, (half + 1) * P)
            nc.vector.scalar_tensor_tensor(
                out=result[:, cols],
                in0=acc_tiles[j][half][:],
                scalar=1.0 / SCALE,
                in1=base[:, j, cols],
                op0=MULT,
                op1=ADD,
            )

        scaled_sums = {}

        def empty_groups(j):
            scaled = out_pool.tile([P, H], F32, name="scaled")
            for half in range(H_HALVES):
                nc.scalar.activation(
                    out=scaled[:, half * P : (half + 1) * P],
                    in_=acc_tiles[j][half][:],
                    func=mybir.ActivationFunctionType.Copy,
                    scale=1.0 / SCALE,
                )
            scaled_sums[j] = scaled

        def add_base_and_store(j):
            result = out_pool.tile([P, H], F32, name="result")
            nc.vector.tensor_tensor(out=result[:], in0=scaled_sums[j][:], in1=base[:, j, :], op=ADD)
            nc.sync.dma_start(out=out_rows[j * P : (j + 1) * P, :], in_=result[:])

        def make_base():
            nc.vector.tensor_reduce(out=count[:], in_=mask_bf[:], axis=mybir.AxisListType.X, op=ADD)
            nc.vector.tensor_scalar(
                out=count_scaled[:], in0=count[:], scalar1=1.0 / SCALE, scalar2=None, op0=MULT
            )
            bias_bank = bank_pool.tile([P, 2 * BANK_UNITS * P], F32, name="bank")
            nc.tensor.matmul(out=bias_bank[:, :H], lhsT=ones[:], rhs=bias_row[:], start=True, stop=True)
            for j in range(NODE_TILES):
                nc.vector.scalar_tensor_tensor(
                    out=base[:, j, :],
                    in0=bias_bank[:, :H],
                    scalar=count_scaled[:, j : j + 1],
                    in1=hv[:, j, :],
                    op0=MULT,
                    op1=ADD,
                )

        mask_and_sort(0)
        transpose_and_group(0)
        mask_and_sort(1)
        make_base()
        for g in range(len(groups)):
            first, n = groups[g]
            if first > 0 and first % EDGES == 0:
                empty_groups(first // EDGES - 1)
            quantise(g)
            if g + 1 == len(groups):
                for j in range(NODE_TILES - 1):
                    add_base_and_store(j)
            if g + 2 < len(groups):
                mask_and_sort(g + 2)
            if g + 1 < len(groups):
                transpose_and_group(g + 1)
            if g + 1 < len(groups):
                multiply(g, range(H_HALVES))
        last_result = out_pool.tile([P, H], F32, name="result")
        for half in range(H_HALVES):
            multiply(len(groups) - 1, [half])
            finish_half(NODE_TILES - 1, half, last_result)
            nc.sync.dma_start(
                out=out_rows[(NODE_TILES - 1) * P :, half * P : (half + 1) * P],
                in_=last_result[:, half * P : (half + 1) * P],
            )
